import numpy as np
import ml_dtypes

BF16 = ml_dtypes.bfloat16


def bf(x):
    return np.asarray(x, np.float32).astype(BF16)


def f32(x):
    return np.asarray(x, np.float32)


def f64(x):
    return np.asarray(x).astype(np.float64)


def striped(idx):
    return np.tile(idx.reshape(-1, 16).T, (8, 1))


C, S, N, T = 256, 512, 1024, 512
ZERO, LEVELS = 8.0, 16


def setup_inputs():
    return {"scales": f32(np.random.uniform(0.05, 0.2, (C, S))), "q": f32(np.random.choice(LEVELS, size=(C, N))), "x": bf(0.2 * np.random.standard_normal((N, T))), "bias": f32(np.random.standard_normal((C, 1))), "residual": f32(np.random.standard_normal((C, T))), "offs": striped(np.random.permutation(np.tile(np.arange(S), 2))[:N])}


def reference(scales, q, x, bias, residual, offs):
    idx = offs[:16].T.reshape(-1)
    w = (f64(q) - ZERO) * f64(scales)[:, idx]
    return w @ f64(x) + f64(bias) + f64(residual)

@@ -1,0 +1,94 @@
+import concourse.mybir as mybir
+from concourse.masks import make_identity
+
+F32, BF16, U16 = mybir.dt.float32, mybir.dt.bfloat16, mybir.dt.uint16
+MULT, ADD = mybir.AluOpType.mult, mybir.AluOpType.add
+COPY = mybir.ActivationFunctionType.Copy
+
+P = 128
+C, S, N, T = 256, 512, 1024, 512
+ZERO_POINT = 8.0
+FEATURE_BLOCKS = C // P
+STEP = 256
+CHANNEL_BLOCKS = STEP // P
+STEPS = N // STEP
+LIST_COLUMNS = STEP // 16
+
+FLOPS = 2 * C * N * T
+
+
+def tile_caigptqlinearop_kernel(tc, scales, q, x, bias, residual, offs, out):
+    nc = tc.nc
+    q_by_block = q.rearrange("(f p) j -> p f j", p=P)
+    x_by_block = x.rearrange("(b p) t -> p b t", p=P)
+    residual_by_block = residual.rearrange("(f p) t -> p f t", p=P)
+
+    with (
+        tc.tile_pool(name="held", bufs=1) as held,
+        tc.tile_pool(name="work", bufs=3) as work,
+        tc.psum_pool(name="flip", bufs=2) as flip,
+        tc.psum_pool(name="sums", bufs=1) as sums,
+    ):
+        offsets = held.tile([P, N // 16], U16, name="offsets")
+        nc.sync.dma_start(offsets[:], offs)
+
+        table = [held.tile([P, S], F32, name=f"table{f}") for f in range(FEATURE_BLOCKS)]
+        levels = [held.tile([P, FEATURE_BLOCKS, STEP], F32, name=f"levels{k}") for k in range(STEPS)]
+        tokens = [held.tile([P, CHANNEL_BLOCKS, T], BF16, name=f"tokens{k}") for k in range(STEPS)]
+
+        def load_levels(k):
+            nc.sync.dma_start(levels[k][:], q_by_block[:, :, k * STEP : (k + 1) * STEP])
+
+        nc.sync.dma_start(table[0][:], scales[0:P, :])
+        load_levels(0)
+        nc.sync.dma_start(table[1][:], scales[P : 2 * P, :])
+        for k in range(STEPS):
+            if k + 1 < STEPS:
+                load_levels(k + 1)
+            nc.sync.dma_start(tokens[k][:], x_by_block[:, k * CHANNEL_BLOCKS : (k + 1) * CHANNEL_BLOCKS, :])
+        bias_column = [held.tile([P, 1], F32, name=f"bias_column{f}") for f in range(FEATURE_BLOCKS)]
+        for f in range(FEATURE_BLOCKS):
+            nc.sync.dma_start(bias_column[f][:], bias[f * P : (f + 1) * P, :])
+        shortcut = held.tile([P, FEATURE_BLOCKS, T], F32, name="shortcut")
+        nc.sync.dma_start(shortcut[:], residual_by_block)
+
+        identity = held.tile([P, P], F32, name="identity")
+        make_identity(nc, identity[:])
+
+        product = [sums.tile([P, T], F32, name=f"product{f}") for f in range(FEATURE_BLOCKS)]
+
+        def dequantise_and_flip(k):
+            nc.scalar.activation(levels[k][:], levels[k][:], COPY, bias=-ZERO_POINT)
+            flipped = flip.tile([P, CHANNEL_BLOCKS, FEATURE_BLOCKS, P], F32, name="flipped")
+            for f in range(FEATURE_BLOCKS):
+                weights = work.tile([P, STEP], F32, name="weights")
+                picked_scales = table[f][:].indirect(offsets[:, k * LIST_COLUMNS : (k + 1) * LIST_COLUMNS])
+                nc.vector.tensor_tensor(weights[:], picked_scales, levels[k][:, f, :], MULT)
+                for b in range(CHANNEL_BLOCKS):
+                    nc.tensor.transpose(flipped[:, b, f, :], weights[:, b * P : (b + 1) * P], identity[:])
+            weights_t = work.tile([P, CHANNEL_BLOCKS, FEATURE_BLOCKS, P], BF16, name="weights_t")
+            nc.scalar.copy(weights_t[:], flipped[:])
+            return weights_t
+
+        def project(k, weights_t):
+            for b in range(CHANNEL_BLOCKS):
+                for f in range(FEATURE_BLOCKS):
+                    nc.tensor.matmul(
+                        product[f][:],
+                        weights_t[:, b, f, :],
+                        tokens[k][:, b, :],
+                        start=(k == 0 and b == 0),
+                        stop=(k == STEPS - 1 and b == CHANNEL_BLOCKS - 1),
+                    )
+
+        earlier = dequantise_and_flip(0)
+        for k in range(1, STEPS):
+            current = dequantise_and_flip(k)
+            project(k - 1, earlier)
+            earlier = current
+        project(STEPS - 1, earlier)
+
+        for f in range(FEATURE_BLOCKS):
+            result = work.tile([P, T], F32, name="result")
+            nc.vector.scalar_tensor_tensor(result[:], product[f][:], bias_column[f][:], shortcut[:, f, :], ADD, ADD)
+            nc.sync.dma_start(out[f * P : (f + 1) * P, :], result[:])

@@ -9,86 +9,94 @@ P = 128
 C, S, N, T = 256, 512, 1024, 512
 ZERO_POINT = 8.0
 FEATURE_BLOCKS = C // P
-STEP = 256
-CHANNEL_BLOCKS = STEP // P
-STEPS = N // STEP
-LIST_COLUMNS = STEP // 16
+PIECE = 256
+CHANNEL_BLOCKS = PIECE // P
+PIECES = N // PIECE
+LIST_COLUMNS = PIECE // 16
+STEPS = FEATURE_BLOCKS * PIECES
+CENTRE_AHEAD = 3
+PROJECT_BEHIND = 2
+WARM_UP_MATMULS = 8
 
 FLOPS = 2 * C * N * T
 
 
 def tile_caigptqlinearop_kernel(tc, scales, q, x, bias, residual, offs, out):
     nc = tc.nc
-    q_by_block = q.rearrange("(f p) j -> p f j", p=P)
     x_by_block = x.rearrange("(b p) t -> p b t", p=P)
-    residual_by_block = residual.rearrange("(f p) t -> p f t", p=P)
 
     with (
         tc.tile_pool(name="held", bufs=1) as held,
-        tc.tile_pool(name="work", bufs=3) as work,
-        tc.psum_pool(name="flip", bufs=2) as flip,
+        tc.tile_pool(name="work", bufs=4) as work,
+        tc.psum_pool(name="flip", bufs=4) as flip,
         tc.psum_pool(name="sums", bufs=1) as sums,
     ):
         offsets = held.tile([P, N // 16], U16, name="offsets")
         nc.sync.dma_start(offsets[:], offs)
 
         table = [held.tile([P, S], F32, name=f"table{f}") for f in range(FEATURE_BLOCKS)]
-        levels = [held.tile([P, FEATURE_BLOCKS, STEP], F32, name=f"levels{k}") for k in range(STEPS)]
-        tokens = [held.tile([P, CHANNEL_BLOCKS, T], BF16, name=f"tokens{k}") for k in range(STEPS)]
-
-        def load_levels(k):
-            nc.sync.dma_start(levels[k][:], q_by_block[:, :, k * STEP : (k + 1) * STEP])
-
-        nc.sync.dma_start(table[0][:], scales[0:P, :])
-        load_levels(0)
-        nc.sync.dma_start(table[1][:], scales[P : 2 * P, :])
-        for k in range(STEPS):
-            if k + 1 < STEPS:
-                load_levels(k + 1)
-            nc.sync.dma_start(tokens[k][:], x_by_block[:, k * CHANNEL_BLOCKS : (k + 1) * CHANNEL_BLOCKS, :])
+        levels = [held.tile([P, PIECE], F32, name=f"levels{s}") for s in range(STEPS)]
+        tokens = [held.tile([P, CHANNEL_BLOCKS, T], BF16, name=f"tokens{k}") for k in range(PIECES)]
+        for s in range(STEPS):
+            f, k = divmod(s, PIECES)
+            nc.sync.dma_start(levels[s][:], q[f * P : (f + 1) * P, k * PIECE : (k + 1) * PIECE])
+            if k == 0:
+                nc.sync.dma_start(table[f][:], scales[f * P : (f + 1) * P, :])
+            if 0 <= s - CENTRE_AHEAD < PIECES:
+                k = s - CENTRE_AHEAD
+                nc.sync.dma_start(tokens[k][:], x_by_block[:, k * CHANNEL_BLOCKS : (k + 1) * CHANNEL_BLOCKS, :])
         bias_column = [held.tile([P, 1], F32, name=f"bias_column{f}") for f in range(FEATURE_BLOCKS)]
+        shortcut = [held.tile([P, T], F32, name=f"shortcut{f}") for f in range(FEATURE_BLOCKS)]
         for f in range(FEATURE_BLOCKS):
             nc.sync.dma_start(bias_column[f][:], bias[f * P : (f + 1) * P, :])
-        shortcut = held.tile([P, FEATURE_BLOCKS, T], F32, name="shortcut")
-        nc.sync.dma_start(shortcut[:], residual_by_block)
+            nc.sync.dma_start(shortcut[f][:], residual[f * P : (f + 1) * P, :])
+
+        zeros = held.tile([P, T], BF16, name="zeros")
+        nc.vector.memset(zeros[:], 0.0)
+        unread = sums.tile([P, T], F32, name="unread")
+        for i in range(WARM_UP_MATMULS):
+            nc.tensor.matmul(unread[:], zeros[:, 0:P], zeros[:], start=(i == 0), stop=(i == WARM_UP_MATMULS - 1))
 
         identity = held.tile([P, P], F32, name="identity")
         make_identity(nc, identity[:])
 
         product = [sums.tile([P, T], F32, name=f"product{f}") for f in range(FEATURE_BLOCKS)]
+        weights_t = [None] * STEPS
 
-        def dequantise_and_flip(k):
-            nc.scalar.activation(levels[k][:], levels[k][:], COPY, bias=-ZERO_POINT)
-            flipped = flip.tile([P, CHANNEL_BLOCKS, FEATURE_BLOCKS, P], F32, name="flipped")
-            for f in range(FEATURE_BLOCKS):
-                weights = work.tile([P, STEP], F32, name="weights")
-                picked_scales = table[f][:].indirect(offsets[:, k * LIST_COLUMNS : (k + 1) * LIST_COLUMNS])
-                nc.vector.tensor_tensor(weights[:], picked_scales, levels[k][:, f, :], MULT)
-                for b in range(CHANNEL_BLOCKS):
-                    nc.tensor.transpose(flipped[:, b, f, :], weights[:, b * P : (b + 1) * P], identity[:])
-            weights_t = work.tile([P, CHANNEL_BLOCKS, FEATURE_BLOCKS, P], BF16, name="weights_t")
-            nc.scalar.copy(weights_t[:], flipped[:])
-            return weights_t
+        def centre(s):
+            nc.scalar.activation(levels[s][:], levels[s][:], COPY, bias=-ZERO_POINT)
 
-        def project(k, weights_t):
+        def dequantise_and_flip(s):
+            f, k = divmod(s, PIECES)
+            weights = work.tile([P, PIECE], F32, name="weights")
+            picked_scales = table[f][:].indirect(offsets[:, k * LIST_COLUMNS : (k + 1) * LIST_COLUMNS])
+            nc.vector.tensor_tensor(weights[:], picked_scales, levels[s][:], MULT)
+            flipped = flip.tile([P, CHANNEL_BLOCKS, P], F32, name="flipped")
             for b in range(CHANNEL_BLOCKS):
-                for f in range(FEATURE_BLOCKS):
-                    nc.tensor.matmul(
-                        product[f][:],
-                        weights_t[:, b, f, :],
-                        tokens[k][:, b, :],
-                        start=(k == 0 and b == 0),
-                        stop=(k == STEPS - 1 and b == CHANNEL_BLOCKS - 1),
-                    )
+                nc.tensor.transpose(flipped[:, b, :], weights[:, b * P : (b + 1) * P], identity[:])
+            weights_t[s] = work.tile([P, CHANNEL_BLOCKS, P], BF16, name="weights_t")
+            nc.scalar.copy(weights_t[s][:], flipped[:])
 
-        earlier = dequantise_and_flip(0)
-        for k in range(1, STEPS):
-            current = dequantise_and_flip(k)
-            project(k - 1, earlier)
-            earlier = current
-        project(STEPS - 1, earlier)
+        def project(s):
+            f, k = divmod(s, PIECES)
+            for b in range(CHANNEL_BLOCKS):
+                nc.tensor.matmul(
+                    product[f][:],
+                    weights_t[s][:, b, :],
+                    tokens[k][:, b, :],
+                    start=(k == 0 and b == 0),
+                    stop=(k == PIECES - 1 and b == CHANNEL_BLOCKS - 1),
+                )
+
+        for r in range(STEPS + CENTRE_AHEAD + PROJECT_BEHIND):
+            if r < STEPS:
+                centre(r)
+            if 0 <= r - CENTRE_AHEAD < STEPS:
+                dequantise_and_flip(r - CENTRE_AHEAD)
+            if 0 <= r - CENTRE_AHEAD - PROJECT_BEHIND:
+                project(r - CENTRE_AHEAD - PROJECT_BEHIND)
 
         for f in range(FEATURE_BLOCKS):
             result = work.tile([P, T], F32, name="result")
-            nc.vector.scalar_tensor_tensor(result[:], product[f][:], bias_column[f][:], shortcut[:, f, :], ADD, ADD)
+            nc.vector.scalar_tensor_tensor(result[:], product[f][:], bias_column[f][:], shortcut[f][:], ADD, ADD)
             nc.sync.dma_start(out[f * P : (f + 1) * P, :], result[:])

@@ -54,8 +54,12 @@ def tile_caigptqlinearop_kernel(tc, scales, q, x, bias, residual, offs, out):
         zeros = held.tile([P, T], BF16, name="zeros")
         nc.vector.memset(zeros[:], 0.0)
         unread = sums.tile([P, T], F32, name="unread")
+
+        def multiply_zeros():
+            nc.tensor.matmul(unread[:], zeros[:, 0:P], zeros[:], start=True, stop=True)
+
         for i in range(WARM_UP_MATMULS):
-            nc.tensor.matmul(unread[:], zeros[:, 0:P], zeros[:], start=(i == 0), stop=(i == WARM_UP_MATMULS - 1))
+            multiply_zeros()
 
         identity = held.tile([P, P], F32, name="identity")
         make_identity(nc, identity[:])
@@ -95,6 +99,8 @@ def tile_caigptqlinearop_kernel(tc, scales, q, x, bias, residual, offs, out):
                 dequantise_and_flip(r - CENTRE_AHEAD)
             if 0 <= r - CENTRE_AHEAD - PROJECT_BEHIND:
                 project(r - CENTRE_AHEAD - PROJECT_BEHIND)
+            elif CENTRE_AHEAD <= r:
+                multiply_zeros()
 
         for f in range(FEATURE_BLOCKS):
             result = work.tile([P, T], F32, name="result")

@@ -16,7 +16,6 @@ LIST_COLUMNS = PIECE // 16
 STEPS = FEATURE_BLOCKS * PIECES
 CENTRE_AHEAD = 3
 PROJECT_BEHIND = 2
-WARM_UP_MATMULS = 8
 
 FLOPS = 2 * C * N * T
 
@@ -50,16 +49,6 @@ def tile_caigptqlinearop_kernel(tc, scales, q, x, bias, residual, offs, out):
         for f in range(FEATURE_BLOCKS):
             nc.sync.dma_start(bias_column[f][:], bias[f * P : (f + 1) * P, :])
             nc.sync.dma_start(shortcut[f][:], residual[f * P : (f + 1) * P, :])
-
-        zeros = held.tile([P, T], BF16, name="zeros")
-        nc.vector.memset(zeros[:], 0.0)
-        unread = sums.tile([P, T], F32, name="unread")
-
-        def multiply_zeros():
-            nc.tensor.matmul(unread[:], zeros[:, 0:P], zeros[:], start=True, stop=True)
-
-        for i in range(WARM_UP_MATMULS):
-            multiply_zeros()
 
         identity = held.tile([P, P], F32, name="identity")
         make_identity(nc, identity[:])
@@ -99,8 +88,6 @@ def tile_caigptqlinearop_kernel(tc, scales, q, x, bias, residual, offs, out):
                 dequantise_and_flip(r - CENTRE_AHEAD)
             if 0 <= r - CENTRE_AHEAD - PROJECT_BEHIND:
                 project(r - CENTRE_AHEAD - PROJECT_BEHIND)
-            elif CENTRE_AHEAD <= r:
-                multiply_zeros()
 
         for f in range(FEATURE_BLOCKS):
             result = work.tile([P, T], F32, name="result")

@@ -14,6 +14,8 @@ CHANNEL_BLOCKS = PIECE // P
 PIECES = N // PIECE
 LIST_COLUMNS = PIECE // 16
 STEPS = FEATURE_BLOCKS * PIECES
+STEPS_PER_LOAD = 2
+Q_LOADS = STEPS // STEPS_PER_LOAD
 CENTRE_AHEAD = 3
 PROJECT_BEHIND = 2
 
@@ -34,16 +36,21 @@ def tile_caigptqlinearop_kernel(tc, scales, q, x, bias, residual, offs, out):
         nc.sync.dma_start(offsets[:], offs)
 
         table = [held.tile([P, S], F32, name=f"table{f}") for f in range(FEATURE_BLOCKS)]
-        levels = [held.tile([P, PIECE], F32, name=f"levels{s}") for s in range(STEPS)]
+        levels = [held.tile([P, STEPS_PER_LOAD * PIECE], F32, name=f"levels{u}") for u in range(Q_LOADS)]
         tokens = [held.tile([P, CHANNEL_BLOCKS, T], BF16, name=f"tokens{k}") for k in range(PIECES)]
-        for s in range(STEPS):
-            f, k = divmod(s, PIECES)
-            nc.sync.dma_start(levels[s][:], q[f * P : (f + 1) * P, k * PIECE : (k + 1) * PIECE])
-            if k == 0:
+
+        def load_tokens(k):
+            nc.sync.dma_start(tokens[k][:], x_by_block[:, k * CHANNEL_BLOCKS : (k + 1) * CHANNEL_BLOCKS, :])
+
+        for u in range(Q_LOADS):
+            f, half = divmod(u, Q_LOADS // FEATURE_BLOCKS)
+            width = STEPS_PER_LOAD * PIECE
+            nc.sync.dma_start(levels[u][:], q[f * P : (f + 1) * P, half * width : (half + 1) * width])
+            if half == 0:
                 nc.sync.dma_start(table[f][:], scales[f * P : (f + 1) * P, :])
-            if 0 <= s - CENTRE_AHEAD < PIECES:
-                k = s - CENTRE_AHEAD
-                nc.sync.dma_start(tokens[k][:], x_by_block[:, k * CHANNEL_BLOCKS : (k + 1) * CHANNEL_BLOCKS, :])
+            if u >= 1:
+                load_tokens(u - 1)
+        load_tokens(PIECES - 1)
         bias_column = [held.tile([P, 1], F32, name=f"bias_column{f}") for f in range(FEATURE_BLOCKS)]
         shortcut = [held.tile([P, T], F32, name=f"shortcut{f}") for f in range(FEATURE_BLOCKS)]
         for f in range(FEATURE_BLOCKS):
@@ -56,14 +63,15 @@ def tile_caigptqlinearop_kernel(tc, scales, q, x, bias, residual, offs, out):
         product = [sums.tile([P, T], F32, name=f"product{f}") for f in range(FEATURE_BLOCKS)]
         weights_t = [None] * STEPS
 
-        def centre(s):
-            nc.scalar.activation(levels[s][:], levels[s][:], COPY, bias=-ZERO_POINT)
+        def centre(u):
+            nc.scalar.activation(levels[u][:], levels[u][:], COPY, bias=-ZERO_POINT)
 
         def dequantise_and_flip(s):
             f, k = divmod(s, PIECES)
+            u, part = divmod(s, STEPS_PER_LOAD)
             weights = work.tile([P, PIECE], F32, name="weights")
             picked_scales = table[f][:].indirect(offsets[:, k * LIST_COLUMNS : (k + 1) * LIST_COLUMNS])
-            nc.vector.tensor_tensor(weights[:], picked_scales, levels[s][:], MULT)
+            nc.vector.tensor_tensor(weights[:], picked_scales, levels[u][:, part * PIECE : (part + 1) * PIECE], MULT)
             flipped = flip.tile([P, CHANNEL_BLOCKS, P], F32, name="flipped")
             for b in range(CHANNEL_BLOCKS):
                 nc.tensor.transpose(flipped[:, b, :], weights[:, b * P : (b + 1) * P], identity[:])
@@ -82,8 +90,8 @@ def tile_caigptqlinearop_kernel(tc, scales, q, x, bias, residual, offs, out):
                 )
 
         for r in range(STEPS + CENTRE_AHEAD + PROJECT_BEHIND):
-            if r < STEPS:
-                centre(r)
+            if r < STEPS and r % STEPS_PER_LOAD == 0:
+                centre(r // STEPS_PER_LOAD)
             if 0 <= r - CENTRE_AHEAD < STEPS:
                 dequantise_and_flip(r - CENTRE_AHEAD)
             if 0 <= r - CENTRE_AHEAD - PROJECT_BEHIND:

@@ -14,10 +14,9 @@ CHANNEL_BLOCKS = PIECE // P
 PIECES = N // PIECE
 LIST_COLUMNS = PIECE // 16
 STEPS = FEATURE_BLOCKS * PIECES
-STEPS_PER_LOAD = 2
-Q_LOADS = STEPS // STEPS_PER_LOAD
 CENTRE_AHEAD = 3
 PROJECT_BEHIND = 2
+X_BEHIND_Q = 4
 
 FLOPS = 2 * C * N * T
 
@@ -36,21 +35,16 @@ def tile_caigptqlinearop_kernel(tc, scales, q, x, bias, residual, offs, out):
         nc.sync.dma_start(offsets[:], offs)
 
         table = [held.tile([P, S], F32, name=f"table{f}") for f in range(FEATURE_BLOCKS)]
-        levels = [held.tile([P, STEPS_PER_LOAD * PIECE], F32, name=f"levels{u}") for u in range(Q_LOADS)]
+        levels = [held.tile([P, PIECE], F32, name=f"levels{s}") for s in range(STEPS)]
         tokens = [held.tile([P, CHANNEL_BLOCKS, T], BF16, name=f"tokens{k}") for k in range(PIECES)]
-
-        def load_tokens(k):
-            nc.sync.dma_start(tokens[k][:], x_by_block[:, k * CHANNEL_BLOCKS : (k + 1) * CHANNEL_BLOCKS, :])
-
-        for u in range(Q_LOADS):
-            f, half = divmod(u, Q_LOADS // FEATURE_BLOCKS)
-            width = STEPS_PER_LOAD * PIECE
-            nc.sync.dma_start(levels[u][:], q[f * P : (f + 1) * P, half * width : (half + 1) * width])
-            if half == 0:
+        for s in range(STEPS):
+            f, k = divmod(s, PIECES)
+            nc.sync.dma_start(levels[s][:], q[f * P : (f + 1) * P, k * PIECE : (k + 1) * PIECE])
+            if k == 0:
                 nc.sync.dma_start(table[f][:], scales[f * P : (f + 1) * P, :])
-            if u >= 1:
-                load_tokens(u - 1)
-        load_tokens(PIECES - 1)
+            if 0 <= s - X_BEHIND_Q < PIECES:
+                k = s - X_BEHIND_Q
+                nc.sync.dma_start(tokens[k][:], x_by_block[:, k * CHANNEL_BLOCKS : (k + 1) * CHANNEL_BLOCKS, :])
         bias_column = [held.tile([P, 1], F32, name=f"bias_column{f}") for f in range(FEATURE_BLOCKS)]
         shortcut = [held.tile([P, T], F32, name=f"shortcut{f}") for f in range(FEATURE_BLOCKS)]
         for f in range(FEATURE_BLOCKS):
@@ -63,15 +57,14 @@ def tile_caigptqlinearop_kernel(tc, scales, q, x, bias, residual, offs, out):
         product = [sums.tile([P, T], F32, name=f"product{f}") for f in range(FEATURE_BLOCKS)]
         weights_t = [None] * STEPS
 
-        def centre(u):
-            nc.scalar.activation(levels[u][:], levels[u][:], COPY, bias=-ZERO_POINT)
+        def centre(s):
+            nc.scalar.activation(levels[s][:], levels[s][:], COPY, bias=-ZERO_POINT)
 
         def dequantise_and_flip(s):
             f, k = divmod(s, PIECES)
-            u, part = divmod(s, STEPS_PER_LOAD)
             weights = work.tile([P, PIECE], F32, name="weights")
             picked_scales = table[f][:].indirect(offsets[:, k * LIST_COLUMNS : (k + 1) * LIST_COLUMNS])
-            nc.vector.tensor_tensor(weights[:], picked_scales, levels[u][:, part * PIECE : (part + 1) * PIECE], MULT)
+            nc.vector.tensor_tensor(weights[:], picked_scales, levels[s][:], MULT)
             flipped = flip.tile([P, CHANNEL_BLOCKS, P], F32, name="flipped")
             for b in range(CHANNEL_BLOCKS):
                 nc.tensor.transpose(flipped[:, b, :], weights[:, b * P : (b + 1) * P], identity[:])
@@ -90,14 +83,18 @@ def tile_caigptqlinearop_kernel(tc, scales, q, x, bias, residual, offs, out):
                 )
 
         for r in range(STEPS + CENTRE_AHEAD + PROJECT_BEHIND):
-            if r < STEPS and r % STEPS_PER_LOAD == 0:
-                centre(r // STEPS_PER_LOAD)
+            if r < STEPS:
+                centre(r)
             if 0 <= r - CENTRE_AHEAD < STEPS:
                 dequantise_and_flip(r - CENTRE_AHEAD)
             if 0 <= r - CENTRE_AHEAD - PROJECT_BEHIND:
                 project(r - CENTRE_AHEAD - PROJECT_BEHIND)
 
         for f in range(FEATURE_BLOCKS):
-            result = work.tile([P, T], F32, name="result")
-            nc.vector.scalar_tensor_tensor(result[:], product[f][:], bias_column[f][:], shortcut[f][:], ADD, ADD)
-            nc.sync.dma_start(out[f * P : (f + 1) * P, :], result[:])
+            for half, queue in enumerate((nc.sync, nc.scalar)):
+                columns = slice(half * (T // 2), (half + 1) * (T // 2))
+                result = work.tile([P, T // 2], F32, name="result")
+                nc.vector.scalar_tensor_tensor(
+                    result[:], product[f][:, columns], bias_column[f][:], shortcut[f][:, columns], ADD, ADD
+                )
+                queue.dma_start(out[f * P : (f + 1) * P, columns], result[:])

@@ -17,6 +17,7 @@ STEPS = FEATURE_BLOCKS * PIECES
 CENTRE_AHEAD = 3
 PROJECT_BEHIND = 2
 X_BEHIND_Q = 4
+WARM_UP_MATMULS = 8
 
 FLOPS = 2 * C * N * T
 
@@ -50,6 +51,12 @@ def tile_caigptqlinearop_kernel(tc, scales, q, x, bias, residual, offs, out):
         for f in range(FEATURE_BLOCKS):
             nc.sync.dma_start(bias_column[f][:], bias[f * P : (f + 1) * P, :])
             nc.sync.dma_start(shortcut[f][:], residual[f * P : (f + 1) * P, :])
+
+        zeros = held.tile([P, T], BF16, name="zeros")
+        nc.vector.memset(zeros[:], 0.0)
+        unread = sums.tile([P, T], F32, name="unread")
+        for i in range(WARM_UP_MATMULS):
+            nc.tensor.matmul(unread[:], zeros[:, 0:P], zeros[:], start=(i == 0), stop=(i == WARM_UP_MATMULS - 1))
 
         identity = held.tile([P, P], F32, name="identity")
         make_identity(nc, identity[:])

@@ -13,10 +13,10 @@ PIECE = 256
 CHANNEL_BLOCKS = PIECE // P
 PIECES = N // PIECE
 LIST_COLUMNS = PIECE // 16
-STEPS = FEATURE_BLOCKS * PIECES
+STEPS = PIECES * FEATURE_BLOCKS
 CENTRE_AHEAD = 3
 PROJECT_BEHIND = 2
-X_BEHIND_Q = 4
+X_BEHIND_Q = 2
 WARM_UP_MATMULS = 8
 
 FLOPS = 2 * C * N * T
@@ -38,13 +38,14 @@ def tile_caigptqlinearop_kernel(tc, scales, q, x, bias, residual, offs, out):
         table = [held.tile([P, S], F32, name=f"table{f}") for f in range(FEATURE_BLOCKS)]
         levels = [held.tile([P, PIECE], F32, name=f"levels{s}") for s in range(STEPS)]
         tokens = [held.tile([P, CHANNEL_BLOCKS, T], BF16, name=f"tokens{k}") for k in range(PIECES)]
-        for s in range(STEPS):
-            f, k = divmod(s, PIECES)
-            nc.sync.dma_start(levels[s][:], q[f * P : (f + 1) * P, k * PIECE : (k + 1) * PIECE])
-            if k == 0:
-                nc.sync.dma_start(table[f][:], scales[f * P : (f + 1) * P, :])
-            if 0 <= s - X_BEHIND_Q < PIECES:
-                k = s - X_BEHIND_Q
+        for s in range(STEPS + X_BEHIND_Q):
+            if s < STEPS:
+                k, f = divmod(s, FEATURE_BLOCKS)
+                nc.sync.dma_start(levels[s][:], q[f * P : (f + 1) * P, k * PIECE : (k + 1) * PIECE])
+                if k == 0:
+                    nc.sync.dma_start(table[f][:], scales[f * P : (f + 1) * P, :])
+            k, f = divmod(s - X_BEHIND_Q, FEATURE_BLOCKS)
+            if k >= 0 and f == FEATURE_BLOCKS - 1:
                 nc.sync.dma_start(tokens[k][:], x_by_block[:, k * CHANNEL_BLOCKS : (k + 1) * CHANNEL_BLOCKS, :])
         bias_column = [held.tile([P, 1], F32, name=f"bias_column{f}") for f in range(FEATURE_BLOCKS)]
         shortcut = [held.tile([P, T], F32, name=f"shortcut{f}") for f in range(FEATURE_BLOCKS)]
@@ -68,7 +69,7 @@ def tile_caigptqlinearop_kernel(tc, scales, q, x, bias, residual, offs, out):
             nc.scalar.activation(levels[s][:], levels[s][:], COPY, bias=-ZERO_POINT)
 
         def dequantise_and_flip(s):
-            f, k = divmod(s, PIECES)
+            k, f = divmod(s, FEATURE_BLOCKS)
             weights = work.tile([P, PIECE], F32, name="weights")
             picked_scales = table[f][:].indirect(offsets[:, k * LIST_COLUMNS : (k + 1) * LIST_COLUMNS])
             nc.vector.tensor_tensor(weights[:], picked_scales, levels[s][:], MULT)
@@ -79,7 +80,7 @@ def tile_caigptqlinearop_kernel(tc, scales, q, x, bias, residual, offs, out):
             nc.scalar.copy(weights_t[s][:], flipped[:])
 
         def project(s):
-            f, k = divmod(s, PIECES)
+            k, f = divmod(s, FEATURE_BLOCKS)
             for b in range(CHANNEL_BLOCKS):
                 nc.tensor.matmul(
                     product[f][:],

@@ -24,7 +24,7 @@ FLOPS = 2 * C * N * T
 
 def tile_caigptqlinearop_kernel(tc, scales, q, x, bias, residual, offs, out):
     nc = tc.nc
-    x_by_block = x.rearrange("(b p) t -> p b t", p=P)
+    x_by_piece = x.rearrange("(k p b) t -> k p b t", p=P, b=CHANNEL_BLOCKS)
 
     with (
         tc.tile_pool(name="held", bufs=1) as held,
@@ -46,7 +46,7 @@ def tile_caigptqlinearop_kernel(tc, scales, q, x, bias, residual, offs, out):
                     nc.sync.dma_start(table[f][:], scales[f * P : (f + 1) * P, :])
             k, f = divmod(s - X_BEHIND_Q, FEATURE_BLOCKS)
             if k >= 0 and f == FEATURE_BLOCKS - 1:
-                nc.sync.dma_start(tokens[k][:], x_by_block[:, k * CHANNEL_BLOCKS : (k + 1) * CHANNEL_BLOCKS, :])
+                nc.sync.dma_start(tokens[k][:], x_by_piece[k])
         bias_column = [held.tile([P, 1], F32, name=f"bias_column{f}") for f in range(FEATURE_BLOCKS)]
         shortcut = [held.tile([P, T], F32, name=f"shortcut{f}") for f in range(FEATURE_BLOCKS)]
         for f in range(FEATURE_BLOCKS):
@@ -75,7 +75,7 @@ def tile_caigptqlinearop_kernel(tc, scales, q, x, bias, residual, offs, out):
             nc.vector.tensor_tensor(weights[:], picked_scales, levels[s][:], MULT)
             flipped = flip.tile([P, CHANNEL_BLOCKS, P], F32, name="flipped")
             for b in range(CHANNEL_BLOCKS):
-                nc.tensor.transpose(flipped[:, b, :], weights[:, b * P : (b + 1) * P], identity[:])
+                nc.tensor.transpose(flipped[:, b, :], weights[:, b:PIECE:CHANNEL_BLOCKS], identity[:])
             weights_t[s] = work.tile([P, CHANNEL_BLOCKS, P], BF16, name="weights_t")
             nc.scalar.copy(weights_t[s][:], flipped[:])
 

@@ -12,10 +12,14 @@ FEATURE_BLOCKS = C // P
 PIECE = 256
 CHANNEL_BLOCKS = PIECE // P
 PIECES = N // PIECE
-LIST_COLUMNS = PIECE // 16
 STEPS = PIECES * FEATURE_BLOCKS
+SPLIT_STEPS = 1
+UNITS = [(s, 0, CHANNEL_BLOCKS) for s in range(STEPS - SPLIT_STEPS)] + [
+    (s, b, 1) for s in range(STEPS - SPLIT_STEPS, STEPS) for b in range(CHANNEL_BLOCKS)
+]
+UNIT_BLOCKS = [(u, b) for u in range(len(UNITS)) for b in range(UNITS[u][2])]
 CENTRE_AHEAD = 3
-PROJECT_BEHIND = 2
+PROJECT_BEHIND = 4
 X_BEHIND_Q = 2
 WARM_UP_MATMULS = 8
 
@@ -24,7 +28,7 @@ FLOPS = 2 * C * N * T
 
 def tile_caigptqlinearop_kernel(tc, scales, q, x, bias, residual, offs, out):
     nc = tc.nc
-    x_by_piece = x.rearrange("(k p b) t -> k p b t", p=P, b=CHANNEL_BLOCKS)
+    x_by_block = x.rearrange("(b p) t -> p b t", p=P)
 
     with (
         tc.tile_pool(name="held", bufs=1) as held,
@@ -33,8 +37,6 @@ def tile_caigptqlinearop_kernel(tc, scales, q, x, bias, residual, offs, out):
         tc.psum_pool(name="sums", bufs=1) as sums,
     ):
         offsets = held.tile([P, N // 16], U16, name="offsets")
-        nc.sync.dma_start(offsets[:], offs)
-
         table = [held.tile([P, S], F32, name=f"table{f}") for f in range(FEATURE_BLOCKS)]
         levels = [held.tile([P, PIECE], F32, name=f"levels{s}") for s in range(STEPS)]
         tokens = [held.tile([P, CHANNEL_BLOCKS, T], BF16, name=f"tokens{k}") for k in range(PIECES)]
@@ -42,11 +44,13 @@ def tile_caigptqlinearop_kernel(tc, scales, q, x, bias, residual, offs, out):
             if s < STEPS:
                 k, f = divmod(s, FEATURE_BLOCKS)
                 nc.sync.dma_start(levels[s][:], q[f * P : (f + 1) * P, k * PIECE : (k + 1) * PIECE])
+                if s == 0:
+                    nc.sync.dma_start(offsets[:], offs)
                 if k == 0:
                     nc.sync.dma_start(table[f][:], scales[f * P : (f + 1) * P, :])
             k, f = divmod(s - X_BEHIND_Q, FEATURE_BLOCKS)
             if k >= 0 and f == FEATURE_BLOCKS - 1:
-                nc.sync.dma_start(tokens[k][:], x_by_piece[k])
+                nc.sync.dma_start(tokens[k][:], x_by_block[:, k * CHANNEL_BLOCKS : (k + 1) * CHANNEL_BLOCKS, :])
         bias_column = [held.tile([P, 1], F32, name=f"bias_column{f}") for f in range(FEATURE_BLOCKS)]
         shortcut = [held.tile([P, T], F32, name=f"shortcut{f}") for f in range(FEATURE_BLOCKS)]
         for f in range(FEATURE_BLOCKS):
@@ -63,40 +67,50 @@ def tile_caigptqlinearop_kernel(tc, scales, q, x, bias, residual, offs, out):
         make_identity(nc, identity[:])
 
         product = [sums.tile([P, T], F32, name=f"product{f}") for f in range(FEATURE_BLOCKS)]
-        weights_t = [None] * STEPS
+        weights_t = [None] * len(UNITS)
 
         def centre(s):
             nc.scalar.activation(levels[s][:], levels[s][:], COPY, bias=-ZERO_POINT)
 
-        def dequantise_and_flip(s):
+        def dequantise_and_flip(u):
+            s, first_block, blocks = UNITS[u]
             k, f = divmod(s, FEATURE_BLOCKS)
-            weights = work.tile([P, PIECE], F32, name="weights")
-            picked_scales = table[f][:].indirect(offsets[:, k * LIST_COLUMNS : (k + 1) * LIST_COLUMNS])
-            nc.vector.tensor_tensor(weights[:], picked_scales, levels[s][:], MULT)
-            flipped = flip.tile([P, CHANNEL_BLOCKS, P], F32, name="flipped")
-            for b in range(CHANNEL_BLOCKS):
-                nc.tensor.transpose(flipped[:, b, :], weights[:, b:PIECE:CHANNEL_BLOCKS], identity[:])
-            weights_t[s] = work.tile([P, CHANNEL_BLOCKS, P], BF16, name="weights_t")
-            nc.scalar.copy(weights_t[s][:], flipped[:])
+            first_in_list = k * PIECE + first_block * P
+            weights = work.tile([P, blocks * P], F32, name="weights")
+            picked_scales = table[f][:].indirect(offsets[:, first_in_list // 16 : (first_in_list + blocks * P) // 16])
+            nc.vector.tensor_tensor(
+                weights[:], picked_scales, levels[s][:, first_block * P : (first_block + blocks) * P], MULT
+            )
+            flipped = flip.tile([P, blocks, P], F32, name="flipped")
+            for b in range(blocks):
+                nc.tensor.transpose(flipped[:, b, :], weights[:, b * P : (b + 1) * P], identity[:])
+            weights_t[u] = work.tile([P, blocks, P], BF16, name="weights_t")
+            nc.scalar.copy(weights_t[u][:], flipped[:])
 
-        def project(s):
+        def project(i):
+            u, b = UNIT_BLOCKS[i]
+            s, first_block, blocks = UNITS[u]
             k, f = divmod(s, FEATURE_BLOCKS)
-            for b in range(CHANNEL_BLOCKS):
-                nc.tensor.matmul(
-                    product[f][:],
-                    weights_t[s][:, b, :],
-                    tokens[k][:, b, :],
-                    start=(k == 0 and b == 0),
-                    stop=(k == PIECES - 1 and b == CHANNEL_BLOCKS - 1),
-                )
+            nc.tensor.matmul(
+                product[f][:],
+                weights_t[u][:, b, :],
+                tokens[k][:, first_block + b, :],
+                start=(k == 0 and first_block + b == 0),
+                stop=(k == PIECES - 1 and first_block + b == CHANNEL_BLOCKS - 1),
+            )
 
-        for r in range(STEPS + CENTRE_AHEAD + PROJECT_BEHIND):
+        flipped, projected = 0, 0
+        for r in range(len(UNITS) + CENTRE_AHEAD):
             if r < STEPS:
                 centre(r)
-            if 0 <= r - CENTRE_AHEAD < STEPS:
+            if r >= CENTRE_AHEAD:
                 dequantise_and_flip(r - CENTRE_AHEAD)
-            if 0 <= r - CENTRE_AHEAD - PROJECT_BEHIND:
-                project(r - CENTRE_AHEAD - PROJECT_BEHIND)
+                flipped += UNITS[r - CENTRE_AHEAD][2]
+            while projected + PROJECT_BEHIND < flipped:
+                project(projected)
+                projected += 1
+        for i in range(projected, len(UNIT_BLOCKS)):
+            project(i)
 
         for f in range(FEATURE_BLOCKS):
             for half, queue in enumerate((nc.sync, nc.scalar)):

@@ -33,7 +33,8 @@ def tile_caigptqlinearop_kernel(tc, scales, q, x, bias, residual, offs, out):
     with (
         tc.tile_pool(name="held", bufs=1) as held,
         tc.tile_pool(name="work", bufs=4) as work,
-        tc.psum_pool(name="flip", bufs=4) as flip,
+        tc.tile_pool(name="flipped_blocks", bufs=2 * PROJECT_BEHIND) as flipped_blocks,
+        tc.psum_pool(name="flip", bufs=5) as flip,
         tc.psum_pool(name="sums", bufs=1) as sums,
     ):
         offsets = held.tile([P, N // 16], U16, name="offsets")
@@ -67,7 +68,7 @@ def tile_caigptqlinearop_kernel(tc, scales, q, x, bias, residual, offs, out):
         make_identity(nc, identity[:])
 
         product = [sums.tile([P, T], F32, name=f"product{f}") for f in range(FEATURE_BLOCKS)]
-        weights_t = [None] * len(UNITS)
+        weights_t = []
 
         def centre(s):
             nc.scalar.activation(levels[s][:], levels[s][:], COPY, bias=-ZERO_POINT)
@@ -81,11 +82,12 @@ def tile_caigptqlinearop_kernel(tc, scales, q, x, bias, residual, offs, out):
             nc.vector.tensor_tensor(
                 weights[:], picked_scales, levels[s][:, first_block * P : (first_block + blocks) * P], MULT
             )
-            flipped = flip.tile([P, blocks, P], F32, name="flipped")
             for b in range(blocks):
-                nc.tensor.transpose(flipped[:, b, :], weights[:, b * P : (b + 1) * P], identity[:])
-            weights_t[u] = work.tile([P, blocks, P], BF16, name="weights_t")
-            nc.scalar.copy(weights_t[u][:], flipped[:])
+                flipped = flip.tile([P, P], F32, name="flipped")
+                nc.tensor.transpose(flipped[:], weights[:, b * P : (b + 1) * P], identity[:])
+                block_t = flipped_blocks.tile([P, P], BF16, name="block_t")
+                nc.scalar.copy(block_t[:], flipped[:])
+                weights_t.append(block_t)
 
         def project(i):
             u, b = UNIT_BLOCKS[i]
@@ -93,7 +95,7 @@ def tile_caigptqlinearop_kernel(tc, scales, q, x, bias, residual, offs, out):
             k, f = divmod(s, FEATURE_BLOCKS)
             nc.tensor.matmul(
                 product[f][:],
-                weights_t[u][:, b, :],
+                weights_t[i][:],
                 tokens[k][:, first_block + b, :],
                 start=(k == 0 and first_block + b == 0),
                 stop=(k == PIECES - 1 and first_block + b == CHANNEL_BLOCKS - 1),

@@ -12,14 +12,10 @@ FEATURE_BLOCKS = C // P
 PIECE = 256
 CHANNEL_BLOCKS = PIECE // P
 PIECES = N // PIECE
+LIST_COLUMNS = PIECE // 16
 STEPS = PIECES * FEATURE_BLOCKS
-SPLIT_STEPS = 1
-UNITS = [(s, 0, CHANNEL_BLOCKS) for s in range(STEPS - SPLIT_STEPS)] + [
-    (s, b, 1) for s in range(STEPS - SPLIT_STEPS, STEPS) for b in range(CHANNEL_BLOCKS)
-]
-UNIT_BLOCKS = [(u, b) for u in range(len(UNITS)) for b in range(UNITS[u][2])]
-CENTRE_AHEAD = 3
-PROJECT_BEHIND = 4
+CENTRE_AHEAD = 2
+PROJECT_BEHIND = 3
 X_BEHIND_Q = 2
 WARM_UP_MATMULS = 8
 
@@ -73,16 +69,12 @@ def tile_caigptqlinearop_kernel(tc, scales, q, x, bias, residual, offs, out):
         def centre(s):
             nc.scalar.activation(levels[s][:], levels[s][:], COPY, bias=-ZERO_POINT)
 
-        def dequantise_and_flip(u):
-            s, first_block, blocks = UNITS[u]
+        def dequantise_and_flip(s):
             k, f = divmod(s, FEATURE_BLOCKS)
-            first_in_list = k * PIECE + first_block * P
-            weights = work.tile([P, blocks * P], F32, name="weights")
-            picked_scales = table[f][:].indirect(offsets[:, first_in_list // 16 : (first_in_list + blocks * P) // 16])
-            nc.vector.tensor_tensor(
-                weights[:], picked_scales, levels[s][:, first_block * P : (first_block + blocks) * P], MULT
-            )
-            for b in range(blocks):
+            weights = work.tile([P, PIECE], F32, name="weights")
+            picked_scales = table[f][:].indirect(offsets[:, k * LIST_COLUMNS : (k + 1) * LIST_COLUMNS])
+            nc.vector.tensor_tensor(weights[:], picked_scales, levels[s][:], MULT)
+            for b in range(CHANNEL_BLOCKS):
                 flipped = flip.tile([P, P], F32, name="flipped")
                 nc.tensor.transpose(flipped[:], weights[:, b * P : (b + 1) * P], identity[:])
                 block_t = flipped_blocks.tile([P, P], BF16, name="block_t")
@@ -90,28 +82,26 @@ def tile_caigptqlinearop_kernel(tc, scales, q, x, bias, residual, offs, out):
                 weights_t.append(block_t)
 
         def project(i):
-            u, b = UNIT_BLOCKS[i]
-            s, first_block, blocks = UNITS[u]
+            s, b = divmod(i, CHANNEL_BLOCKS)
             k, f = divmod(s, FEATURE_BLOCKS)
             nc.tensor.matmul(
                 product[f][:],
                 weights_t[i][:],
-                tokens[k][:, first_block + b, :],
-                start=(k == 0 and first_block + b == 0),
-                stop=(k == PIECES - 1 and first_block + b == CHANNEL_BLOCKS - 1),
+                tokens[k][:, b, :],
+                start=(k == 0 and b == 0),
+                stop=(k == PIECES - 1 and b == CHANNEL_BLOCKS - 1),
             )
 
-        flipped, projected = 0, 0
-        for r in range(len(UNITS) + CENTRE_AHEAD):
+        projected = 0
+        for r in range(STEPS + CENTRE_AHEAD):
             if r < STEPS:
                 centre(r)
             if r >= CENTRE_AHEAD:
                 dequantise_and_flip(r - CENTRE_AHEAD)
-                flipped += UNITS[r - CENTRE_AHEAD][2]
-            while projected + PROJECT_BEHIND < flipped:
+            while projected + PROJECT_BEHIND < len(weights_t):
                 project(projected)
                 projected += 1
-        for i in range(projected, len(UNIT_BLOCKS)):
+        for i in range(projected, len(weights_t)):
             project(i)
 
         for f in range(FEATURE_BLOCKS):

@@ -17,7 +17,7 @@ STEPS = PIECES * FEATURE_BLOCKS
 CENTRE_AHEAD = 2
 PROJECT_BEHIND = 3
 X_BEHIND_Q = 2
-WARM_UP_MATMULS = 8
+WARM_UP_MATMULS = 11
 
 FLOPS = 2 * C * N * T
 

@@ -14,10 +14,10 @@ CHANNEL_BLOCKS = PIECE // P
 PIECES = N // PIECE
 LIST_COLUMNS = PIECE // 16
 STEPS = PIECES * FEATURE_BLOCKS
-CENTRE_AHEAD = 2
+CENTRE_AHEAD = 4
 PROJECT_BEHIND = 3
 X_BEHIND_Q = 2
-WARM_UP_MATMULS = 11
+WARM_UP_MATMULS = 7
 
 FLOPS = 2 * C * N * T
 
@@ -29,8 +29,9 @@ def tile_caigptqlinearop_kernel(tc, scales, q, x, bias, residual, offs, out):
     with (
         tc.tile_pool(name="held", bufs=1) as held,
         tc.tile_pool(name="work", bufs=4) as work,
+        tc.tile_pool(name="steps", bufs=CENTRE_AHEAD) as steps,
         tc.tile_pool(name="flipped_blocks", bufs=2 * PROJECT_BEHIND) as flipped_blocks,
-        tc.psum_pool(name="flip", bufs=5) as flip,
+        tc.psum_pool(name="flip", bufs=4) as flip,
         tc.psum_pool(name="sums", bufs=1) as sums,
     ):
         offsets = held.tile([P, N // 16], U16, name="offsets")
@@ -64,16 +65,19 @@ def tile_caigptqlinearop_kernel(tc, scales, q, x, bias, residual, offs, out):
         make_identity(nc, identity[:])
 
         product = [sums.tile([P, T], F32, name=f"product{f}") for f in range(FEATURE_BLOCKS)]
+        centred_and_weights = []
         weights_t = []
 
         def centre(s):
-            nc.scalar.activation(levels[s][:], levels[s][:], COPY, bias=-ZERO_POINT)
+            step = steps.tile([P, 2, PIECE], F32, name="step")
+            nc.scalar.activation(step[:, 0, :], levels[s][:], COPY, bias=-ZERO_POINT)
+            centred_and_weights.append(step)
 
         def dequantise_and_flip(s):
             k, f = divmod(s, FEATURE_BLOCKS)
-            weights = work.tile([P, PIECE], F32, name="weights")
+            centred, weights = centred_and_weights[s][:, 0, :], centred_and_weights[s][:, 1, :]
             picked_scales = table[f][:].indirect(offsets[:, k * LIST_COLUMNS : (k + 1) * LIST_COLUMNS])
-            nc.vector.tensor_tensor(weights[:], picked_scales, levels[s][:], MULT)
+            nc.vector.tensor_tensor(weights, picked_scales, centred, MULT)
             for b in range(CHANNEL_BLOCKS):
                 flipped = flip.tile([P, P], F32, name="flipped")
                 nc.tensor.transpose(flipped[:], weights[:, b * P : (b + 1) * P], identity[:])
@@ -94,10 +98,10 @@ def tile_caigptqlinearop_kernel(tc, scales, q, x, bias, residual, offs, out):
 
         projected = 0
         for r in range(STEPS + CENTRE_AHEAD):
-            if r < STEPS:
-                centre(r)
             if r >= CENTRE_AHEAD:
                 dequantise_and_flip(r - CENTRE_AHEAD)
+            if r < STEPS:
+                centre(r)
             while projected + PROJECT_BEHIND < len(weights_t):
                 project(projected)
                 projected += 1

@@ -13,10 +13,13 @@ PIECE = 256
 CHANNEL_BLOCKS = PIECE // P
 PIECES = N // PIECE
 LIST_COLUMNS = PIECE // 16
-STEPS = PIECES * FEATURE_BLOCKS
+STEPS_IN_ORDER = [(k, f) for k in range(PIECES - 2) for f in range(FEATURE_BLOCKS)] + [
+    (k, f) for f in range(FEATURE_BLOCKS) for k in range(PIECES - 2, PIECES)
+]
+STEPS = len(STEPS_IN_ORDER)
 CENTRE_AHEAD = 4
 PROJECT_BEHIND = 3
-X_BEHIND_Q = 2
+X_BEHIND_Q = 3
 WARM_UP_MATMULS = 7
 
 FLOPS = 2 * C * N * T
@@ -40,14 +43,15 @@ def tile_caigptqlinearop_kernel(tc, scales, q, x, bias, residual, offs, out):
         tokens = [held.tile([P, CHANNEL_BLOCKS, T], BF16, name=f"tokens{k}") for k in range(PIECES)]
         for s in range(STEPS + X_BEHIND_Q):
             if s < STEPS:
-                k, f = divmod(s, FEATURE_BLOCKS)
+                k, f = STEPS_IN_ORDER[s]
                 nc.sync.dma_start(levels[s][:], q[f * P : (f + 1) * P, k * PIECE : (k + 1) * PIECE])
                 if s == 0:
                     nc.sync.dma_start(offsets[:], offs)
                 if k == 0:
                     nc.sync.dma_start(table[f][:], scales[f * P : (f + 1) * P, :])
-            k, f = divmod(s - X_BEHIND_Q, FEATURE_BLOCKS)
-            if k >= 0 and f == FEATURE_BLOCKS - 1:
+            first_step = s - X_BEHIND_Q
+            if 0 <= first_step < STEPS and STEPS_IN_ORDER[first_step][1] == 0:
+                k = STEPS_IN_ORDER[first_step][0]
                 nc.sync.dma_start(tokens[k][:], x_by_block[:, k * CHANNEL_BLOCKS : (k + 1) * CHANNEL_BLOCKS, :])
         bias_column = [held.tile([P, 1], F32, name=f"bias_column{f}") for f in range(FEATURE_BLOCKS)]
         shortcut = [held.tile([P, T], F32, name=f"shortcut{f}") for f in range(FEATURE_BLOCKS)]
@@ -64,7 +68,10 @@ def tile_caigptqlinearop_kernel(tc, scales, q, x, bias, residual, offs, out):
         identity = held.tile([P, P], F32, name="identity")
         make_identity(nc, identity[:])
 
-        product = [sums.tile([P, T], F32, name=f"product{f}") for f in range(FEATURE_BLOCKS)]
+        product = [[(sums.tile([P, T], F32, name=f"product{f}"), slice(0, T))] for f in range(FEATURE_BLOCKS - 1)]
+        product.append(
+            [(sums.tile([P, T // 2], F32, name=f"last_product{h}"), slice(h * T // 2, (h + 1) * T // 2)) for h in range(2)]
+        )
         centred_and_weights = []
         weights_t = []
 
@@ -74,7 +81,7 @@ def tile_caigptqlinearop_kernel(tc, scales, q, x, bias, residual, offs, out):
             centred_and_weights.append(step)
 
         def dequantise_and_flip(s):
-            k, f = divmod(s, FEATURE_BLOCKS)
+            k, f = STEPS_IN_ORDER[s]
             centred, weights = centred_and_weights[s][:, 0, :], centred_and_weights[s][:, 1, :]
             picked_scales = table[f][:].indirect(offsets[:, k * LIST_COLUMNS : (k + 1) * LIST_COLUMNS])
             nc.vector.tensor_tensor(weights, picked_scales, centred, MULT)
@@ -85,16 +92,20 @@ def tile_caigptqlinearop_kernel(tc, scales, q, x, bias, residual, offs, out):
                 nc.scalar.copy(block_t[:], flipped[:])
                 weights_t.append(block_t)
 
-        def project(i):
+        def project(i, part):
             s, b = divmod(i, CHANNEL_BLOCKS)
-            k, f = divmod(s, FEATURE_BLOCKS)
+            k, f = STEPS_IN_ORDER[s]
+            sums_tile, columns = product[f][part]
             nc.tensor.matmul(
-                product[f][:],
+                sums_tile[:],
                 weights_t[i][:],
-                tokens[k][:, b, :],
+                tokens[k][:, b, columns],
                 start=(k == 0 and b == 0),
                 stop=(k == PIECES - 1 and b == CHANNEL_BLOCKS - 1),
             )
+
+        def parts_of(i):
+            return range(len(product[STEPS_IN_ORDER[i // CHANNEL_BLOCKS][1]]))
 
         projected = 0
         for r in range(STEPS + CENTRE_AHEAD):
@@ -103,16 +114,24 @@ def tile_caigptqlinearop_kernel(tc, scales, q, x, bias, residual, offs, out):
             if r < STEPS:
                 centre(r)
             while projected + PROJECT_BEHIND < len(weights_t):
-                project(projected)
+                for part in parts_of(projected):
+                    project(projected, part)
                 projected += 1
-        for i in range(projected, len(weights_t)):
-            project(i)
+        last_step = range((STEPS - 1) * CHANNEL_BLOCKS, STEPS * CHANNEL_BLOCKS)
+        for i in range(projected, last_step.start):
+            for part in parts_of(i):
+                project(i, part)
+        for part in parts_of(last_step.start):
+            for i in last_step:
+                project(i, part)
 
         for f in range(FEATURE_BLOCKS):
             for half, queue in enumerate((nc.sync, nc.scalar)):
                 columns = slice(half * (T // 2), (half + 1) * (T // 2))
+                sums_tile, held_columns = product[f][half % len(product[f])]
+                summed = sums_tile[:, columns.start - held_columns.start : columns.stop - held_columns.start]
                 result = work.tile([P, T // 2], F32, name="result")
                 nc.vector.scalar_tensor_tensor(
-                    result[:], product[f][:, columns], bias_column[f][:], shortcut[f][:, columns], ADD, ADD
+                    result[:], summed, bias_column[f][:], shortcut[f][:, columns], ADD, ADD
                 )
                 queue.dma_start(out[f * P : (f + 1) * P, columns], result[:])

@@ -13,13 +13,10 @@ PIECE = 256
 CHANNEL_BLOCKS = PIECE // P
 PIECES = N // PIECE
 LIST_COLUMNS = PIECE // 16
-STEPS_IN_ORDER = [(k, f) for k in range(PIECES - 2) for f in range(FEATURE_BLOCKS)] + [
-    (k, f) for f in range(FEATURE_BLOCKS) for k in range(PIECES - 2, PIECES)
-]
+STEPS_IN_ORDER = [(k, f) for pair in range(PIECES // 2) for f in range(FEATURE_BLOCKS) for k in (2 * pair, 2 * pair + 1)]
 STEPS = len(STEPS_IN_ORDER)
 CENTRE_AHEAD = 4
 PROJECT_BEHIND = 3
-X_BEHIND_Q = 3
 WARM_UP_MATMULS = 7
 
 FLOPS = 2 * C * N * T
@@ -41,18 +38,33 @@ def tile_caigptqlinearop_kernel(tc, scales, q, x, bias, residual, offs, out):
         table = [held.tile([P, S], F32, name=f"table{f}") for f in range(FEATURE_BLOCKS)]
         levels = [held.tile([P, PIECE], F32, name=f"levels{s}") for s in range(STEPS)]
         tokens = [held.tile([P, CHANNEL_BLOCKS, T], BF16, name=f"tokens{k}") for k in range(PIECES)]
-        for s in range(STEPS + X_BEHIND_Q):
-            if s < STEPS:
-                k, f = STEPS_IN_ORDER[s]
-                nc.sync.dma_start(levels[s][:], q[f * P : (f + 1) * P, k * PIECE : (k + 1) * PIECE])
-                if s == 0:
-                    nc.sync.dma_start(offsets[:], offs)
-                if k == 0:
-                    nc.sync.dma_start(table[f][:], scales[f * P : (f + 1) * P, :])
-            first_step = s - X_BEHIND_Q
-            if 0 <= first_step < STEPS and STEPS_IN_ORDER[first_step][1] == 0:
-                k = STEPS_IN_ORDER[first_step][0]
-                nc.sync.dma_start(tokens[k][:], x_by_block[:, k * CHANNEL_BLOCKS : (k + 1) * CHANNEL_BLOCKS, :])
+
+        def load_levels(s):
+            k, f = STEPS_IN_ORDER[s]
+            nc.sync.dma_start(levels[s][:], q[f * P : (f + 1) * P, k * PIECE : (k + 1) * PIECE])
+
+        def load_table(f):
+            nc.sync.dma_start(table[f][:], scales[f * P : (f + 1) * P, :])
+
+        def load_tokens(k, blocks):
+            first = k * CHANNEL_BLOCKS + blocks.start
+            nc.sync.dma_start(tokens[k][:, blocks, :], x_by_block[:, first : first + blocks.stop - blocks.start, :])
+
+        whole_piece = slice(0, CHANNEL_BLOCKS)
+        load_levels(0)
+        load_table(0)
+        nc.sync.dma_start(offsets[:], offs)
+        for s in range(1, 4):
+            load_levels(s)
+        load_table(1)
+        load_tokens(0, whole_piece)
+        for b in range(CHANNEL_BLOCKS):
+            load_levels(4 + b)
+            load_tokens(1, slice(b, b + 1))
+        for s in range(6, STEPS):
+            load_levels(s)
+        for k in range(2, PIECES):
+            load_tokens(k, whole_piece)
         bias_column = [held.tile([P, 1], F32, name=f"bias_column{f}") for f in range(FEATURE_BLOCKS)]
         shortcut = [held.tile([P, T], F32, name=f"shortcut{f}") for f in range(FEATURE_BLOCKS)]
         for f in range(FEATURE_BLOCKS):

@@ -57,18 +57,18 @@ def tile_caigptqlinearop_kernel(tc, scales, q, x, bias, residual, offs, out):
         for s in range(1, 4):
             load_levels(s)
         load_table(1)
-        load_tokens(0, whole_piece)
-        for b in range(CHANNEL_BLOCKS):
-            load_levels(4 + b)
-            load_tokens(1, slice(b, b + 1))
+        for k in range(2):
+            load_tokens(k, slice(0, 1))
+            load_levels(4 + k)
+            load_tokens(k, slice(1, 2))
         for s in range(6, STEPS):
             load_levels(s)
         for k in range(2, PIECES):
             load_tokens(k, whole_piece)
-        bias_column = [held.tile([P, 1], F32, name=f"bias_column{f}") for f in range(FEATURE_BLOCKS)]
+        bias_columns = held.tile([P, FEATURE_BLOCKS], F32, name="bias_columns")
+        nc.sync.dma_start(bias_columns[:], bias.rearrange("(f p) o -> p (f o)", p=P))
         shortcut = [held.tile([P, T], F32, name=f"shortcut{f}") for f in range(FEATURE_BLOCKS)]
         for f in range(FEATURE_BLOCKS):
-            nc.sync.dma_start(bias_column[f][:], bias[f * P : (f + 1) * P, :])
             nc.sync.dma_start(shortcut[f][:], residual[f * P : (f + 1) * P, :])
 
         zeros = held.tile([P, T], BF16, name="zeros")
@@ -144,6 +144,6 @@ def tile_caigptqlinearop_kernel(tc, scales, q, x, bias, residual, offs, out):
                 summed = sums_tile[:, columns.start - held_columns.start : columns.stop - held_columns.start]
                 result = work.tile([P, T // 2], F32, name="result")
                 nc.vector.scalar_tensor_tensor(
-                    result[:], summed, bias_column[f][:], shortcut[f][:, columns], ADD, ADD
+                    result[:], summed, bias_columns[:, f : f + 1], shortcut[f][:, columns], ADD, ADD
                 )
                 queue.dma_start(out[f * P : (f + 1) * P, columns], result[:])

@@ -92,12 +92,14 @@ def tile_caigptqlinearop_kernel(tc, scales, q, x, bias, residual, offs, out):
             nc.scalar.activation(step[:, 0, :], levels[s][:], COPY, bias=-ZERO_POINT)
             centred_and_weights.append(step)
 
-        def dequantise_and_flip(s):
+        def dequantise_and_flip(s, blocks):
             k, f = STEPS_IN_ORDER[s]
             centred, weights = centred_and_weights[s][:, 0, :], centred_and_weights[s][:, 1, :]
-            picked_scales = table[f][:].indirect(offsets[:, k * LIST_COLUMNS : (k + 1) * LIST_COLUMNS])
-            nc.vector.tensor_tensor(weights, picked_scales, centred, MULT)
-            for b in range(CHANNEL_BLOCKS):
+            entries = slice(blocks.start * P, blocks.stop * P)
+            columns = slice(k * LIST_COLUMNS + entries.start // 16, k * LIST_COLUMNS + entries.stop // 16)
+            picked_scales = table[f][:].indirect(offsets[:, columns])
+            nc.vector.tensor_tensor(weights[:, entries], picked_scales, centred[:, entries], MULT)
+            for b in blocks:
                 flipped = flip.tile([P, P], F32, name="flipped")
                 nc.tensor.transpose(flipped[:], weights[:, b * P : (b + 1) * P], identity[:])
                 block_t = flipped_blocks.tile([P, P], BF16, name="block_t")
@@ -121,14 +123,17 @@ def tile_caigptqlinearop_kernel(tc, scales, q, x, bias, residual, offs, out):
 
         projected = 0
         for r in range(STEPS + CENTRE_AHEAD):
-            if r >= CENTRE_AHEAD:
-                dequantise_and_flip(r - CENTRE_AHEAD)
-            if r < STEPS:
-                centre(r)
-            while projected + PROJECT_BEHIND < len(weights_t):
-                for part in parts_of(projected):
-                    project(projected, part)
-                projected += 1
+            last_round = r == STEPS + CENTRE_AHEAD - 1
+            units = [range(b, b + 1) for b in range(CHANNEL_BLOCKS)] if last_round else [range(CHANNEL_BLOCKS)]
+            for blocks in units:
+                if r >= CENTRE_AHEAD:
+                    dequantise_and_flip(r - CENTRE_AHEAD, blocks)
+                if r < STEPS:
+                    centre(r)
+                while projected + PROJECT_BEHIND < len(weights_t):
+                    for part in parts_of(projected):
+                        project(projected, part)
+                    projected += 1
         last_step = range((STEPS - 1) * CHANNEL_BLOCKS, STEPS * CHANNEL_BLOCKS)
         for i in range(projected, last_step.start):
             for part in parts_of(i):

@@ -58,9 +58,9 @@ def tile_caigptqlinearop_kernel(tc, scales, q, x, bias, residual, offs, out):
             load_levels(s)
         load_table(1)
         for k in range(2):
-            load_tokens(k, slice(0, 1))
             load_levels(4 + k)
-            load_tokens(k, slice(1, 2))
+            for b in range(CHANNEL_BLOCKS):
+                load_tokens(k, slice(b, b + 1))
         for s in range(6, STEPS):
             load_levels(s)
         for k in range(2, PIECES):

@@ -54,9 +54,10 @@ def tile_caigptqlinearop_kernel(tc, scales, q, x, bias, residual, offs, out):
         load_levels(0)
         load_table(0)
         nc.sync.dma_start(offsets[:], offs)
-        for s in range(1, 4):
-            load_levels(s)
+        load_levels(1)
+        load_levels(2)
         load_table(1)
+        load_levels(3)
         for k in range(2):
             load_levels(4 + k)
             for b in range(CHANNEL_BLOCKS):

@@ -58,12 +58,14 @@ def tile_caigptqlinearop_kernel(tc, scales, q, x, bias, residual, offs, out):
         load_levels(2)
         load_table(1)
         load_levels(3)
-        for k in range(2):
-            load_levels(4 + k)
-            for b in range(CHANNEL_BLOCKS):
-                load_tokens(k, slice(b, b + 1))
-        for s in range(6, STEPS):
-            load_levels(s)
+        load_levels(4)
+        for b in range(CHANNEL_BLOCKS):
+            load_tokens(0, slice(b, b + 1))
+        load_levels(5)
+        load_levels(6)
+        for b in range(CHANNEL_BLOCKS):
+            load_tokens(1, slice(b, b + 1))
+        load_levels(7)
         for k in range(2, PIECES):
             load_tokens(k, whole_piece)
         bias_columns = held.tile([P, FEATURE_BLOCKS], F32, name="bias_columns")

import concourse.mybir as mybir
from concourse.masks import make_identity

F32, BF16, U16 = mybir.dt.float32, mybir.dt.bfloat16, mybir.dt.uint16
MULT, ADD = mybir.AluOpType.mult, mybir.AluOpType.add
COPY = mybir.ActivationFunctionType.Copy

P = 128
C, S, N, T = 256, 512, 1024, 512
ZERO_POINT = 8.0
FEATURE_BLOCKS = C // P
PIECE = 256
CHANNEL_BLOCKS = PIECE // P
PIECES = N // PIECE
LIST_COLUMNS = PIECE // 16
STEPS_IN_ORDER = [(k, f) for pair in range(PIECES // 2) for f in range(FEATURE_BLOCKS) for k in (2 * pair, 2 * pair + 1)]
STEPS = len(STEPS_IN_ORDER)
CENTRE_AHEAD = 4
PROJECT_BEHIND = 3
WARM_UP_MATMULS = 7

FLOPS = 2 * C * N * T


def tile_caigptqlinearop_kernel(tc, scales, q, x, bias, residual, offs, out):
    nc = tc.nc
    x_by_block = x.rearrange("(b p) t -> p b t", p=P)

    with (
        tc.tile_pool(name="held", bufs=1) as held,
        tc.tile_pool(name="work", bufs=4) as work,
        tc.tile_pool(name="steps", bufs=CENTRE_AHEAD) as steps,
        tc.tile_pool(name="flipped_blocks", bufs=2 * PROJECT_BEHIND) as flipped_blocks,
        tc.psum_pool(name="flip", bufs=4) as flip,
        tc.psum_pool(name="sums", bufs=1) as sums,
    ):
        offsets = held.tile([P, N // 16], U16, name="offsets")
        table = [held.tile([P, S], F32, name=f"table{f}") for f in range(FEATURE_BLOCKS)]
        levels = [held.tile([P, PIECE], F32, name=f"levels{s}") for s in range(STEPS)]
        tokens = [held.tile([P, CHANNEL_BLOCKS, T], BF16, name=f"tokens{k}") for k in range(PIECES)]

        def load_levels(s):
            k, f = STEPS_IN_ORDER[s]
            nc.sync.dma_start(levels[s][:], q[f * P : (f + 1) * P, k * PIECE : (k + 1) * PIECE])

        def load_table(f):
            nc.sync.dma_start(table[f][:], scales[f * P : (f + 1) * P, :])

        def load_tokens(k, blocks):
            first = k * CHANNEL_BLOCKS + blocks.start
            nc.sync.dma_start(tokens[k][:, blocks, :], x_by_block[:, first : first + blocks.stop - blocks.start, :])

        whole_piece = slice(0, CHANNEL_BLOCKS)
        load_levels(0)
        load_table(0)
        nc.sync.dma_start(offsets[:], offs)
        load_levels(1)
        load_levels(2)
        load_table(1)
        load_levels(3)
        load_levels(4)
        for b in range(CHANNEL_BLOCKS):
            load_tokens(0, slice(b, b + 1))
        load_levels(5)
        load_levels(6)
        for b in range(CHANNEL_BLOCKS):
            load_tokens(1, slice(b, b + 1))
        load_levels(7)
        for k in range(2, PIECES):
            load_tokens(k, whole_piece)
        bias_columns = held.tile([P, FEATURE_BLOCKS], F32, name="bias_columns")
        nc.sync.dma_start(bias_columns[:], bias.rearrange("(f p) o -> p (f o)", p=P))
        shortcut = [held.tile([P, T], F32, name=f"shortcut{f}") for f in range(FEATURE_BLOCKS)]
        for f in range(FEATURE_BLOCKS):
            nc.sync.dma_start(shortcut[f][:], residual[f * P : (f + 1) * P, :])

        zeros = held.tile([P, T], BF16, name="zeros")
        nc.vector.memset(zeros[:], 0.0)
        unread = sums.tile([P, T], F32, name="unread")
        for i in range(WARM_UP_MATMULS):
            nc.tensor.matmul(unread[:], zeros[:, 0:P], zeros[:], start=(i == 0), stop=(i == WARM_UP_MATMULS - 1))

        identity = held.tile([P, P], F32, name="identity")
        make_identity(nc, identity[:])

        product = [[(sums.tile([P, T], F32, name=f"product{f}"), slice(0, T))] for f in range(FEATURE_BLOCKS - 1)]
        product.append(
            [(sums.tile([P, T // 2], F32, name=f"last_product{h}"), slice(h * T // 2, (h + 1) * T // 2)) for h in range(2)]
        )
        centred_and_weights = []
        weights_t = []

        def centre(s):
            step = steps.tile([P, 2, PIECE], F32, name="step")
            nc.scalar.activation(step[:, 0, :], levels[s][:], COPY, bias=-ZERO_POINT)
            centred_and_weights.append(step)

        def dequantise_and_flip(s, blocks):
            k, f = STEPS_IN_ORDER[s]
            centred, weights = centred_and_weights[s][:, 0, :], centred_and_weights[s][:, 1, :]
            entries = slice(blocks.start * P, blocks.stop * P)
            columns = slice(k * LIST_COLUMNS + entries.start // 16, k * LIST_COLUMNS + entries.stop // 16)
            picked_scales = table[f][:].indirect(offsets[:, columns])
            nc.vector.tensor_tensor(weights[:, entries], picked_scales, centred[:, entries], MULT)
            for b in blocks:
                flipped = flip.tile([P, P], F32, name="flipped")
                nc.tensor.transpose(flipped[:], weights[:, b * P : (b + 1) * P], identity[:])
                block_t = flipped_blocks.tile([P, P], BF16, name="block_t")
                nc.scalar.copy(block_t[:], flipped[:])
                weights_t.append(block_t)

        def project(i, part):
            s, b = divmod(i, CHANNEL_BLOCKS)
            k, f = STEPS_IN_ORDER[s]
            sums_tile, columns = product[f][part]
            nc.tensor.matmul(
                sums_tile[:],
                weights_t[i][:],
                tokens[k][:, b, columns],
                start=(k == 0 and b == 0),
                stop=(k == PIECES - 1 and b == CHANNEL_BLOCKS - 1),
            )

        def parts_of(i):
            return range(len(product[STEPS_IN_ORDER[i // CHANNEL_BLOCKS][1]]))

        projected = 0
        for r in range(STEPS + CENTRE_AHEAD):
            last_round = r == STEPS + CENTRE_AHEAD - 1
            units = [range(b, b + 1) for b in range(CHANNEL_BLOCKS)] if last_round else [range(CHANNEL_BLOCKS)]
            for blocks in units:
                if r >= CENTRE_AHEAD:
                    dequantise_and_flip(r - CENTRE_AHEAD, blocks)
                if r < STEPS:
                    centre(r)
                while projected + PROJECT_BEHIND < len(weights_t):
                    for part in parts_of(projected):
                        project(projected, part)
                    projected += 1
        last_step = range((STEPS - 1) * CHANNEL_BLOCKS, STEPS * CHANNEL_BLOCKS)
        for i in range(projected, last_step.start):
            for part in parts_of(i):
                project(i, part)
        for part in parts_of(last_step.start):
            for i in last_step:
                project(i, part)

        for f in range(FEATURE_BLOCKS):
            for half, queue in enumerate((nc.sync, nc.scalar)):
                columns = slice(half * (T // 2), (half + 1) * (T // 2))
                sums_tile, held_columns = product[f][half % len(product[f])]
                summed = sums_tile[:, columns.start - held_columns.start : columns.stop - held_columns.start]
                result = work.tile([P, T // 2], F32, name="result")
                nc.vector.scalar_tensor_tensor(
                    result[:], summed, bias_columns[:, f : f + 1], shortcut[f][:, columns], ADD, ADD
                )
                queue.dma_start(out[f * P : (f + 1) * P, columns], result[:])
